import numpy as np
import ml_dtypes

BF16 = ml_dtypes.bfloat16


def bf(x):
    return np.asarray(x, np.float32).astype(BF16)


def f32(x):
    return np.asarray(x, np.float32)


def f64(x):
    return np.asarray(x).astype(np.float64)


def striped(idx):
    return np.tile(idx.reshape(-1, 16).T, (8, 1))


K, C, S, N = 512, 128, 2048, 1024
DENS = 1.0 / 64.0
SIG_MU, SIG, SIG_BASE = 0.25, 0.2, 0.12


def lift(sp, axis):
    t = np.sqrt(1.0 + np.sum(f64(sp) ** 2, axis=axis, keepdims=True))
    return f32(np.concatenate([t, f64(sp)], axis=axis))


def setup_inputs():
    mu = SIG_MU * np.random.standard_normal((1, C - 1))
    h = lift(f32(mu + SIG * np.random.standard_normal((K, C - 1))), 1)
    mask = (np.random.random_sample((K, N)) < DENS).astype(np.float64)
    mask[np.arange(N) % K, np.arange(N)] = 1.0
    adj_t = bf(mask / np.sum(mask, axis=0, keepdims=True))
    base = lift(f32(SIG_BASE * np.random.standard_normal((C - 1, S))), 0)
    return {"h": h, "adj_t": adj_t, "base": base, "offs": striped(np.random.permutation(S)[:N])}


def reference(h, adj_t, base, offs):
    idx = offs[:16].T.reshape(-1)
    m = f64(h).T @ f64(adj_t)
    q = -m[:1] ** 2 + np.sum(m[1:] ** 2, axis=0, keepdims=True)
    out = f64(base).copy()
    out[:, idx] = m * (1.0 / np.sqrt(np.abs(q)))
    return out

@@ -1,0 +1,71 @@
+import concourse.mybir as mybir
+
+F32 = mybir.dt.float32
+BF16 = mybir.dt.bfloat16
+U16 = mybir.dt.uint16
+MULT = mybir.AluOpType.mult
+SQUARE = mybir.ActivationFunctionType.Square
+ABS_RSQRT = mybir.ActivationFunctionType.Abs_reciprocal_sqrt
+
+P = 128
+SOURCES = 512
+TARGETS = 1024
+STORE = 2048
+K_BLOCKS = SOURCES // P
+PIECE = 512
+PIECES = TARGETS // PIECE
+OFFS_COLS = PIECE // 16
+
+FLOPS = 2 * SOURCES * P * TARGETS + 4 * P * TARGETS
+
+
+def tile_fulllorentzgraphneuralnetwork_kernel(tc, h, adj_t, base, offs, out):
+    nc = tc.nc
+    with (
+        tc.tile_pool(name="held", bufs=1) as held,
+        tc.psum_pool(name="psum", bufs=1) as psum,
+    ):
+        offsets = held.tile([P, TARGETS // 16], U16, name="offsets")
+        nc.sync.dma_start(offsets[:], offs)
+
+        h_f32 = held.tile([P, K_BLOCKS, P], F32, name="h_f32")
+        nc.scalar.dma_start(h_f32[:], h.rearrange("(p k) c -> p k c", k=K_BLOCKS))
+
+        adj_blocks = adj_t.rearrange("(p k) j -> p k j", k=K_BLOCKS)
+        adj = []
+        for piece in range(PIECES):
+            adj_piece = held.tile([P, K_BLOCKS, PIECE], BF16, name=f"adj{piece}")
+            nc.sync.dma_start(adj_piece[:], adj_blocks[:, :, piece * PIECE : (piece + 1) * PIECE])
+            adj.append(adj_piece)
+
+        window = held.tile([P, STORE], F32, name="window")
+        nc.scalar.dma_start(window[:], base)
+
+        minkowski = held.tile([P, P], BF16, name="minkowski")
+        nc.vector.memset(minkowski[:], 1.0)
+        nc.vector.memset(minkowski[0:1, :], -1.0)
+
+        h_bf16 = held.tile([P, K_BLOCKS, P], BF16, name="h_bf16")
+        nc.vector.tensor_copy(h_bf16[:], h_f32[:])
+
+        for piece in range(PIECES):
+            m_psum = psum.tile([P, PIECE], F32, name=f"m_psum{piece}")
+            for k in range(K_BLOCKS):
+                nc.tensor.matmul(
+                    m_psum[:], h_bf16[:, k, :], adj[piece][:, k, :], start=(k == 0), stop=(k == K_BLOCKS - 1)
+                )
+
+            squares = held.tile([P, PIECE], BF16, name=f"squares{piece}")
+            nc.scalar.activation(squares[:], m_psum[:], SQUARE)
+            m_sbuf = held.tile([P, PIECE], F32, name=f"m_sbuf{piece}")
+            nc.vector.tensor_copy(m_sbuf[:], m_psum[:])
+
+            q_psum = psum.tile([P, PIECE], F32, name=f"q_psum{piece}")
+            nc.tensor.matmul(q_psum[:], minkowski[:], squares[:], start=True, stop=True)
+            inv_norm = held.tile([P, PIECE], F32, name=f"inv_norm{piece}")
+            nc.scalar.activation(inv_norm[:], q_psum[:], ABS_RSQRT)
+
+            piece_offsets = offsets[:, piece * OFFS_COLS : (piece + 1) * OFFS_COLS]
+            nc.vector.tensor_tensor(window[:].indirect(piece_offsets), m_sbuf[:], inv_norm[:], MULT)
+
+        nc.sync.dma_start(out, window[:])

@@ -45,6 +45,10 @@ def tile_fulllorentzgraphneuralnetwork_kernel(tc, h, adj_t, base, offs, out):
         nc.vector.memset(minkowski[:], 1.0)
         nc.vector.memset(minkowski[0:1, :], -1.0)
 
+        scratch = held.tile([P, 1], F32, name="scratch")
+        nc.vector.memset(scratch[:], 1.0)
+        nc.scalar.activation(scratch[:], scratch[:], ABS_RSQRT)
+
         h_bf16 = held.tile([P, K_BLOCKS, P], BF16, name="h_bf16")
         nc.vector.tensor_copy(h_bf16[:], h_f32[:])
 

@@ -15,6 +15,7 @@ K_BLOCKS = SOURCES // P
 PIECE = 512
 PIECES = TARGETS // PIECE
 OFFS_COLS = PIECE // 16
+WARM_MATMULS = 24
 
 FLOPS = 2 * SOURCES * P * TARGETS + 4 * P * TARGETS
 
@@ -45,6 +46,10 @@ def tile_fulllorentzgraphneuralnetwork_kernel(tc, h, adj_t, base, offs, out):
         nc.vector.memset(minkowski[:], 1.0)
         nc.vector.memset(minkowski[0:1, :], -1.0)
 
+        warm_psum = psum.tile([P, P], F32, name="warm_psum")
+        for repeat in range(WARM_MATMULS):
+            nc.tensor.matmul(warm_psum[:], minkowski[:], minkowski[:], start=True, stop=True)
+
         scratch = held.tile([P, 1], F32, name="scratch")
         nc.vector.memset(scratch[:], 1.0)
         nc.scalar.activation(scratch[:], scratch[:], ABS_RSQRT)
@@ -62,7 +67,10 @@ def tile_fulllorentzgraphneuralnetwork_kernel(tc, h, adj_t, base, offs, out):
             squares = held.tile([P, PIECE], BF16, name=f"squares{piece}")
             nc.scalar.activation(squares[:], m_psum[:], SQUARE)
             m_sbuf = held.tile([P, PIECE], F32, name=f"m_sbuf{piece}")
-            nc.vector.tensor_copy(m_sbuf[:], m_psum[:])
+            if piece == 0:
+                nc.vector.tensor_copy(m_sbuf[:], m_psum[:])
+            else:
+                nc.scalar.copy(m_sbuf[:], m_psum[:])
 
             q_psum = psum.tile([P, PIECE], F32, name=f"q_psum{piece}")
             nc.tensor.matmul(q_psum[:], minkowski[:], squares[:], start=True, stop=True)

@@ -26,21 +26,19 @@ def tile_fulllorentzgraphneuralnetwork_kernel(tc, h, adj_t, base, offs, out):
         tc.tile_pool(name="held", bufs=1) as held,
         tc.psum_pool(name="psum", bufs=1) as psum,
     ):
-        offsets = held.tile([P, TARGETS // 16], U16, name="offsets")
-        nc.sync.dma_start(offsets[:], offs)
-
         h_f32 = held.tile([P, K_BLOCKS, P], F32, name="h_f32")
-        nc.scalar.dma_start(h_f32[:], h.rearrange("(p k) c -> p k c", k=K_BLOCKS))
+        nc.sync.dma_start(h_f32[:], h.rearrange("(p k) c -> p k c", k=K_BLOCKS))
 
         adj_blocks = adj_t.rearrange("(p k) j -> p k j", k=K_BLOCKS)
-        adj = []
-        for piece in range(PIECES):
-            adj_piece = held.tile([P, K_BLOCKS, PIECE], BF16, name=f"adj{piece}")
-            nc.sync.dma_start(adj_piece[:], adj_blocks[:, :, piece * PIECE : (piece + 1) * PIECE])
-            adj.append(adj_piece)
-
+        adj = [[held.tile([P, PIECE], BF16, name=f"adj{piece}_{k}") for k in range(K_BLOCKS)] for piece in range(PIECES)]
+        offsets = held.tile([P, TARGETS // 16], U16, name="offsets")
         window = held.tile([P, STORE], F32, name="window")
-        nc.scalar.dma_start(window[:], base)
+        for piece in range(PIECES):
+            for k in range(K_BLOCKS):
+                nc.sync.dma_start(adj[piece][k][:], adj_blocks[:, k, piece * PIECE : (piece + 1) * PIECE])
+            if piece == 0:
+                nc.sync.dma_start(offsets[:], offs)
+                nc.sync.dma_start(window[:], base)
 
         minkowski = held.tile([P, P], BF16, name="minkowski")
         nc.vector.memset(minkowski[:], 1.0)
@@ -58,21 +56,18 @@ def tile_fulllorentzgraphneuralnetwork_kernel(tc, h, adj_t, base, offs, out):
         nc.vector.tensor_copy(h_bf16[:], h_f32[:])
 
         for piece in range(PIECES):
-            m_psum = psum.tile([P, PIECE], F32, name=f"m_psum{piece}")
+            m_psum = psum.tile([P, PIECE], F32, name="m_psum")
             for k in range(K_BLOCKS):
                 nc.tensor.matmul(
-                    m_psum[:], h_bf16[:, k, :], adj[piece][:, k, :], start=(k == 0), stop=(k == K_BLOCKS - 1)
+                    m_psum[:], h_bf16[:, k, :], adj[piece][k][:], start=(k == 0), stop=(k == K_BLOCKS - 1)
                 )
 
             squares = held.tile([P, PIECE], BF16, name=f"squares{piece}")
             nc.scalar.activation(squares[:], m_psum[:], SQUARE)
             m_sbuf = held.tile([P, PIECE], F32, name=f"m_sbuf{piece}")
-            if piece == 0:
-                nc.vector.tensor_copy(m_sbuf[:], m_psum[:])
-            else:
-                nc.scalar.copy(m_sbuf[:], m_psum[:])
+            nc.scalar.copy(m_sbuf[:], m_psum[:])
 
-            q_psum = psum.tile([P, PIECE], F32, name=f"q_psum{piece}")
+            q_psum = psum.tile([P, PIECE], F32, name="q_psum")
             nc.tensor.matmul(q_psum[:], minkowski[:], squares[:], start=True, stop=True)
             inv_norm = held.tile([P, PIECE], F32, name=f"inv_norm{piece}")
             nc.scalar.activation(inv_norm[:], q_psum[:], ABS_RSQRT)

@@ -15,7 +15,6 @@ K_BLOCKS = SOURCES // P
 PIECE = 512
 PIECES = TARGETS // PIECE
 OFFS_COLS = PIECE // 16
-WARM_MATMULS = 24
 
 FLOPS = 2 * SOURCES * P * TARGETS + 4 * P * TARGETS
 
@@ -43,10 +42,6 @@ def tile_fulllorentzgraphneuralnetwork_kernel(tc, h, adj_t, base, offs, out):
         minkowski = held.tile([P, P], BF16, name="minkowski")
         nc.vector.memset(minkowski[:], 1.0)
         nc.vector.memset(minkowski[0:1, :], -1.0)
-
-        warm_psum = psum.tile([P, P], F32, name="warm_psum")
-        for repeat in range(WARM_MATMULS):
-            nc.tensor.matmul(warm_psum[:], minkowski[:], minkowski[:], start=True, stop=True)
 
         scratch = held.tile([P, 1], F32, name="scratch")
         nc.vector.memset(scratch[:], 1.0)

@@ -15,6 +15,8 @@ K_BLOCKS = SOURCES // P
 PIECE = 512
 PIECES = TARGETS // PIECE
 OFFS_COLS = PIECE // 16
+HALVES = 2
+HALF = PIECE // HALVES
 
 FLOPS = 2 * SOURCES * P * TARGETS + 4 * P * TARGETS
 
@@ -57,15 +59,20 @@ def tile_fulllorentzgraphneuralnetwork_kernel(tc, h, adj_t, base, offs, out):
                     m_psum[:], h_bf16[:, k, :], adj[piece][k][:], start=(k == 0), stop=(k == K_BLOCKS - 1)
                 )
 
-            squares = held.tile([P, PIECE], BF16, name=f"squares{piece}")
-            nc.scalar.activation(squares[:], m_psum[:], SQUARE)
+            q_psum = []
+            for half in range(HALVES):
+                squares = held.tile([P, HALF], BF16, name=f"squares{piece}_{half}")
+                nc.scalar.activation(squares[:], m_psum[:, half * HALF : (half + 1) * HALF], SQUARE)
+                q_half = psum.tile([P, HALF], F32, name=f"q_psum{half}")
+                nc.tensor.matmul(q_half[:], minkowski[:], squares[:], start=True, stop=True)
+                q_psum.append(q_half)
+
             m_sbuf = held.tile([P, PIECE], F32, name=f"m_sbuf{piece}")
             nc.scalar.copy(m_sbuf[:], m_psum[:])
 
-            q_psum = psum.tile([P, PIECE], F32, name="q_psum")
-            nc.tensor.matmul(q_psum[:], minkowski[:], squares[:], start=True, stop=True)
             inv_norm = held.tile([P, PIECE], F32, name=f"inv_norm{piece}")
-            nc.scalar.activation(inv_norm[:], q_psum[:], ABS_RSQRT)
+            for half in range(HALVES):
+                nc.scalar.activation(inv_norm[:, half * HALF : (half + 1) * HALF], q_psum[half][:], ABS_RSQRT)
 
             piece_offsets = offsets[:, piece * OFFS_COLS : (piece + 1) * OFFS_COLS]
             nc.vector.tensor_tensor(window[:].indirect(piece_offsets), m_sbuf[:], inv_norm[:], MULT)

@@ -16,6 +16,7 @@ PIECE = 512
 PIECES = TARGETS // PIECE
 OFFS_COLS = PIECE // 16
 HALVES = 2
+WARM_MATMULS = 12
 HALF = PIECE // HALVES
 
 FLOPS = 2 * SOURCES * P * TARGETS + 4 * P * TARGETS
@@ -44,6 +45,10 @@ def tile_fulllorentzgraphneuralnetwork_kernel(tc, h, adj_t, base, offs, out):
         minkowski = held.tile([P, P], BF16, name="minkowski")
         nc.vector.memset(minkowski[:], 1.0)
         nc.vector.memset(minkowski[0:1, :], -1.0)
+
+        warm_psum = psum.tile([P, P], F32, name="warm_psum")
+        for repeat in range(WARM_MATMULS):
+            nc.tensor.matmul(warm_psum[:], minkowski[:], minkowski[:], start=True, stop=True)
 
         scratch = held.tile([P, 1], F32, name="scratch")
         nc.vector.memset(scratch[:], 1.0)

@@ -16,8 +16,8 @@ PIECE = 512
 PIECES = TARGETS // PIECE
 OFFS_COLS = PIECE // 16
 HALVES = 2
-WARM_MATMULS = 12
 HALF = PIECE // HALVES
+WARM_MATMULS = 12
 
 FLOPS = 2 * SOURCES * P * TARGETS + 4 * P * TARGETS
 
@@ -54,30 +54,33 @@ def tile_fulllorentzgraphneuralnetwork_kernel(tc, h, adj_t, base, offs, out):
         nc.vector.memset(scratch[:], 1.0)
         nc.scalar.activation(scratch[:], scratch[:], ABS_RSQRT)
 
-        h_bf16 = held.tile([P, K_BLOCKS, P], BF16, name="h_bf16")
-        nc.vector.tensor_copy(h_bf16[:], h_f32[:])
+        h_bf16 = [held.tile([P, P], BF16, name=f"h_bf16_{k}") for k in range(K_BLOCKS)]
+        for k in range(K_BLOCKS):
+            nc.vector.tensor_copy(h_bf16[k][:], h_f32[:, k, :])
 
         for piece in range(PIECES):
-            m_psum = psum.tile([P, PIECE], F32, name="m_psum")
-            for k in range(K_BLOCKS):
-                nc.tensor.matmul(
-                    m_psum[:], h_bf16[:, k, :], adj[piece][k][:], start=(k == 0), stop=(k == K_BLOCKS - 1)
-                )
-
-            q_psum = []
-            for half in range(HALVES):
-                squares = held.tile([P, HALF], BF16, name=f"squares{piece}_{half}")
-                nc.scalar.activation(squares[:], m_psum[:, half * HALF : (half + 1) * HALF], SQUARE)
-                q_half = psum.tile([P, HALF], F32, name=f"q_psum{half}")
-                nc.tensor.matmul(q_half[:], minkowski[:], squares[:], start=True, stop=True)
-                q_psum.append(q_half)
-
             m_sbuf = held.tile([P, PIECE], F32, name=f"m_sbuf{piece}")
-            nc.scalar.copy(m_sbuf[:], m_psum[:])
-
             inv_norm = held.tile([P, PIECE], F32, name=f"inv_norm{piece}")
             for half in range(HALVES):
-                nc.scalar.activation(inv_norm[:, half * HALF : (half + 1) * HALF], q_psum[half][:], ABS_RSQRT)
+                columns = slice(half * HALF, (half + 1) * HALF)
+
+                m_psum = psum.tile([P, HALF], F32, name=f"m_psum{piece}_{half}")
+                for k in range(K_BLOCKS):
+                    nc.tensor.matmul(
+                        m_psum[:], h_bf16[k][:], adj[piece][k][:, columns], start=(k == 0), stop=(k == K_BLOCKS - 1)
+                    )
+
+                squares = held.tile([P, HALF], BF16, name=f"squares{piece}_{half}")
+                nc.scalar.activation(squares[:], m_psum[:], SQUARE)
+                q_psum = psum.tile([P, HALF], F32, name=f"q_psum{half}")
+                nc.tensor.matmul(q_psum[:], minkowski[:], squares[:], start=True, stop=True)
+
+                if piece == 0:
+                    nc.vector.tensor_copy(m_sbuf[:, columns], m_psum[:])
+                else:
+                    nc.scalar.copy(m_sbuf[:, columns], m_psum[:])
+
+                nc.scalar.activation(inv_norm[:, columns], q_psum[:], ABS_RSQRT)
 
             piece_offsets = offsets[:, piece * OFFS_COLS : (piece + 1) * OFFS_COLS]
             nc.vector.tensor_tensor(window[:].indirect(piece_offsets), m_sbuf[:], inv_norm[:], MULT)

import concourse.mybir as mybir

F32 = mybir.dt.float32
BF16 = mybir.dt.bfloat16
U16 = mybir.dt.uint16
MULT = mybir.AluOpType.mult
SQUARE = mybir.ActivationFunctionType.Square
ABS_RSQRT = mybir.ActivationFunctionType.Abs_reciprocal_sqrt

P = 128
SOURCES = 512
TARGETS = 1024
STORE = 2048
K_BLOCKS = SOURCES // P
PIECE = 512
PIECES = TARGETS // PIECE
OFFS_COLS = PIECE // 16
HALVES = 2
HALF = PIECE // HALVES
WARM_MATMULS = 12

FLOPS = 2 * SOURCES * P * TARGETS + 4 * P * TARGETS


def tile_fulllorentzgraphneuralnetwork_kernel(tc, h, adj_t, base, offs, out):
    nc = tc.nc
    with (
        tc.tile_pool(name="held", bufs=1) as held,
        tc.psum_pool(name="psum", bufs=1) as psum,
    ):
        h_f32 = held.tile([P, K_BLOCKS, P], F32, name="h_f32")
        nc.sync.dma_start(h_f32[:], h.rearrange("(p k) c -> p k c", k=K_BLOCKS))

        adj_blocks = adj_t.rearrange("(p k) j -> p k j", k=K_BLOCKS)
        adj = [[held.tile([P, PIECE], BF16, name=f"adj{piece}_{k}") for k in range(K_BLOCKS)] for piece in range(PIECES)]
        offsets = held.tile([P, TARGETS // 16], U16, name="offsets")
        window = held.tile([P, STORE], F32, name="window")
        for piece in range(PIECES):
            for k in range(K_BLOCKS):
                nc.sync.dma_start(adj[piece][k][:], adj_blocks[:, k, piece * PIECE : (piece + 1) * PIECE])
            if piece == 0:
                nc.sync.dma_start(offsets[:], offs)
                nc.sync.dma_start(window[:], base)

        minkowski = held.tile([P, P], BF16, name="minkowski")
        nc.vector.memset(minkowski[:], 1.0)
        nc.vector.memset(minkowski[0:1, :], -1.0)

        warm_psum = psum.tile([P, P], F32, name="warm_psum")
        for repeat in range(WARM_MATMULS):
            nc.tensor.matmul(warm_psum[:], minkowski[:], minkowski[:], start=True, stop=True)

        scratch = held.tile([P, 1], F32, name="scratch")
        nc.vector.memset(scratch[:], 1.0)
        nc.scalar.activation(scratch[:], scratch[:], ABS_RSQRT)

        h_bf16 = [held.tile([P, P], BF16, name=f"h_bf16_{k}") for k in range(K_BLOCKS)]
        for k in range(K_BLOCKS):
            nc.vector.tensor_copy(h_bf16[k][:], h_f32[:, k, :])

        for piece in range(PIECES):
            m_sbuf = held.tile([P, PIECE], F32, name=f"m_sbuf{piece}")
            inv_norm = held.tile([P, PIECE], F32, name=f"inv_norm{piece}")
            for half in range(HALVES):
                columns = slice(half * HALF, (half + 1) * HALF)

                m_psum = psum.tile([P, HALF], F32, name=f"m_psum{piece}_{half}")
                for k in range(K_BLOCKS):
                    nc.tensor.matmul(
                        m_psum[:], h_bf16[k][:], adj[piece][k][:, columns], start=(k == 0), stop=(k == K_BLOCKS - 1)
                    )

                squares = held.tile([P, HALF], BF16, name=f"squares{piece}_{half}")
                nc.scalar.activation(squares[:], m_psum[:], SQUARE)
                q_psum = psum.tile([P, HALF], F32, name=f"q_psum{half}")
                nc.tensor.matmul(q_psum[:], minkowski[:], squares[:], start=True, stop=True)

                if piece == 0:
                    nc.vector.tensor_copy(m_sbuf[:, columns], m_psum[:])
                else:
                    nc.scalar.copy(m_sbuf[:, columns], m_psum[:])

                nc.scalar.activation(inv_norm[:, columns], q_psum[:], ABS_RSQRT)

            piece_offsets = offsets[:, piece * OFFS_COLS : (piece + 1) * OFFS_COLS]
            nc.vector.tensor_tensor(window[:].indirect(piece_offsets), m_sbuf[:], inv_norm[:], MULT)

        nc.sync.dma_start(out, window[:])
